import numpy as np
import ml_dtypes


def mxq(x, axis, fmt="e4m3"):
    dtype, down = {"e4m3": (ml_dtypes.float8_e4m3fn, 7), "e5m2": (ml_dtypes.float8_e5m2, 14)}[fmt]
    v = np.moveaxis(np.asarray(x, np.float32).astype(ml_dtypes.bfloat16).astype(np.float64), axis, -1)
    blocks = v.reshape(v.shape[:-1] + (-1, 32))
    amax = np.abs(blocks).max(-1, keepdims=True)
    byte = np.maximum(np.where(amax > 0, np.frexp(amax)[1] - 1 + 127, 0) - down, 1)
    scale = np.exp2(byte - 127.0)
    codes = (blocks / scale).astype(np.float32).astype(dtype).astype(np.float64)
    return np.moveaxis((codes * scale).reshape(v.shape), -1, axis)


WIDE = False


def mx_kscale(k):
    if not WIDE:
        return np.ones(k)
    levels = np.array([10, -10, 5, -5, 0])
    a = np.random.permutation(np.resize(levels, k // 512 * 4)).reshape(k // 512, 4)
    idx = np.arange(k)
    return np.exp2(a[idx // 512, idx % 128 // 32])


BF16 = ml_dtypes.bfloat16


def bf(x):
    return np.asarray(x, np.float32).astype(BF16)


def f64(x):
    return np.asarray(x).astype(np.float64)


E2M1 = np.array([0.0, 0.5, 1.0, 1.5, 2.0, 3.0, 4.0, 6.0, -0.0, -0.5, -1.0, -1.5, -2.0, -3.0, -4.0, -6.0])


def pack_weight(w, fmt):
    k, n = w.shape
    w = f64(bf(w)).reshape(k // 32, 32, n)
    amax = np.abs(w).max(1)
    if fmt == "e4m3":
        byte = np.frexp(amax)[1] - 1 + 127 - 7
    else:
        mant, ex = np.frexp(amax / 6.0)
        byte = np.where(mant > 0.5, ex, ex - 1) + 127
    byte = np.clip(np.where(amax > 0, byte, 1), 1, 254)
    scaled = (w * np.exp2(127.0 - byte)[:, None, :]).reshape(k, n).astype(np.float32)
    by_word = np.ascontiguousarray(scaled.reshape(k // 512, 128, 4, n).transpose(0, 1, 3, 2))
    if fmt == "e4m3":
        words = by_word.astype(ml_dtypes.float8_e4m3fn).view(np.uint8)
    else:
        c = by_word.astype(ml_dtypes.float4_e2m1fn).view(np.uint8) & 0xF
        words = c[..., 0::2] | (c[..., 1::2] << 4)
    return np.ascontiguousarray(words), np.ascontiguousarray(byte.astype(np.uint8).reshape(k // 512, 16, n))


def unpack_weight(words, scales, fmt):
    g, p, n, _ = words.shape
    if fmt == "e4m3":
        vals = np.ascontiguousarray(words).view(ml_dtypes.float8_e4m3fn).astype(np.float64)
    else:
        nib = np.empty((g, p, n, 4), np.uint8)
        nib[..., 0::2] = words & 0xF
        nib[..., 1::2] = words >> 4
        vals = E2M1[nib]
    vals = vals * np.repeat(np.exp2(scales.astype(np.float64) - 127.0), 8, axis=1)[..., None]
    return vals.transpose(0, 1, 3, 2).reshape(g * 512, n)


B, L, S, D, DA, H, MLP = 2, 3, 128, 1024, 16384, 16, 4096
EPS = 1e-5


def layer_norm(u, g, b):
    mu = u.mean(-1, keepdims=True)
    var = ((u - mu) ** 2).mean(-1, keepdims=True)
    return (u - mu) / np.sqrt(var + EPS) * g + b


def setup_inputs():
    s = mx_kscale(DA)
    r = np.random.standard_normal
    h_attn = bf(r((B, S, DA)) * 2.0 * s)
    x = bf(r((B, S, D)))
    words, scales = pack_weight(r((DA, D)) * 0.5 / np.sqrt(DA) / s[:, None], "e4m3")
    return {"h_attn": h_attn, "x": x,
            "attn_out_W_words": words, "attn_out_W_scales": scales, "attn_out_b": bf(r(D) * 0.2),
            "attn_norm_g": bf(1.0 + 0.1 * r(D)), "attn_norm_b": bf(r(D) * 0.1)}


def reference(h_attn, x, attn_out_W_words, attn_out_W_scales, attn_out_b, attn_norm_g, attn_norm_b):
    o = (mxq(f64(h_attn), 2, "e4m3") @ unpack_weight(attn_out_W_words, attn_out_W_scales, "e4m3")) + f64(attn_out_b)
    return f64(x) + layer_norm(o, f64(attn_norm_g), f64(attn_norm_b))

@@ -1,0 +1,217 @@
+from contextlib import ExitStack
+
+import concourse.mybir as mybir
+from concourse.masks import make_identity
+
+FP8X4 = mybir.dt.float8_e4m3fn_x4
+BF16 = mybir.dt.bfloat16
+F32 = mybir.dt.float32
+I32 = mybir.dt.int32
+U32 = mybir.dt.uint32
+U8 = mybir.dt.uint8
+ALU = mybir.AluOpType
+ACT = mybir.ActivationFunctionType
+
+P = 128
+BATCH = 2
+K = 16384
+N = 1024
+PACK = 4
+K_PASS = P * PACK
+PASSES = K // K_PASS
+HALF = 512
+HALVES = N // HALF
+CHUNK = 4
+CHUNKS = PASSES // CHUNK
+WORDS_PASS = K_PASS // 2
+QUADRANTS = 4
+EPS = 1e-5
+
+FLOPS = 2 * BATCH * P * K * N
+
+
+def tile_dcadecoderblock_pb_k_kernel(
+    tc, h_attn, x, w_words, w_scales, proj_bias, norm_gain, norm_shift, out
+):
+    nc = tc.nc
+    with ExitStack() as ctx:
+        keep = ctx.enter_context(tc.tile_pool(name="keep", bufs=1))
+        h_pool = ctx.enter_context(tc.tile_pool(name="h_pool", bufs=3))
+        grouped_pool = ctx.enter_context(tc.tile_pool(name="grouped_pool", bufs=2))
+        w_pool = ctx.enter_context(tc.tile_pool(name="w_pool", bufs=5 * CHUNK))
+        acc_pool = ctx.enter_context(tc.psum_pool(name="acc_pool", bufs=1))
+        bank_pool = ctx.enter_context(tc.psum_pool(name="bank_pool", bufs=4))
+        ctx.enter_context(tc.manual_schedule())
+
+        ident = keep.tile([P, P], F32)
+        ones = keep.tile([P, P], BF16)
+        rows = keep.tile([P, 3, N], BF16)
+        spread = keep.tile([P, 3, N], F32)
+        x_sb = keep.tile([P, BATCH, N], BF16)
+        shift_x = keep.tile([P, BATCH, N], F32)
+        w_planes = keep.tile([P, CHUNKS, N], U8, align_bytes=64)
+        h_codes = keep.tile([P, PASSES * BATCH * P], U32, align_bytes=64)
+        h_planes = keep.tile([P, PASSES * BATCH * P], U8, align_bytes=64)
+        eps_col = keep.tile([P, 1], F32)
+        warm = keep.tile([P, 1], F32)
+
+        nc.vector.memset(w_planes[:].rearrange("p c n -> p (c n)").bitcast(I32), 0)
+        nc.vector.memset(rows[:], 0.0)
+        nc.vector.memset(ones[:], 1.0)
+        nc.vector.memset(eps_col[:], EPS)
+        make_identity(nc, ident[:])
+        for v, vec in enumerate((proj_bias, norm_gain, norm_shift)):
+            nc.scalar.dma_start(out=rows[0:1, v, :], in_=vec.unsqueeze(0))
+        nc.scalar.activation(out=warm[:], in_=eps_col[:], func=ACT.Sqrt)
+
+        h_view = h_attn.rearrange("b s k -> s b k")
+        h_raw = []
+        w_sb = []
+
+        def load_h(c):
+            raw = h_pool.tile([P, BATCH, CHUNK * K_PASS], BF16, name="raw")
+            k_cols = slice(c * CHUNK * K_PASS, (c + 1) * CHUNK * K_PASS)
+            nc.sync.dma_start(out=raw[:], in_=h_view[:, :, k_cols])
+            h_raw.append(raw)
+
+        def load_w(c):
+            for q in range(QUADRANTS):
+                nc.sync.dma_start(
+                    out=w_planes[32 * q : 32 * q + 4 * CHUNK, c, :].bitcast(I32),
+                    in_=w_scales[CHUNK * c : CHUNK * (c + 1), 4 * q : 4 * q + 4, :].bitcast(I32),
+                )
+            for g in range(CHUNK * c, CHUNK * (c + 1)):
+                words = w_pool.tile([P, N], U32, name="words", align_bytes=64)
+                nc.sync.dma_start(
+                    out=words[:].bitcast(I32),
+                    in_=w_words[g].rearrange("p n t -> p (n t)").bitcast(I32),
+                )
+                w_sb.append(words)
+
+        load_h(0)
+        load_h(1)
+        for c in range(CHUNKS):
+            load_w(c)
+            if c + 2 < CHUNKS:
+                load_h(c + 2)
+            if c == CHUNKS // 2:
+                nc.sync.dma_start(out=x_sb[:], in_=x.rearrange("b s n -> s b n"))
+
+        acc = [
+            [acc_pool.tile([P, HALF], F32, name="acc%d%d" % (b, j)) for j in range(HALVES)]
+            for b in range(BATCH)
+        ]
+
+        def transpose_chunk(c):
+            grouped = grouped_pool.tile([P, CHUNK * BATCH * P * PACK], BF16, name="grouped", align_bytes=64)
+            grouped_words = grouped[:].bitcast(F32)
+            for i in range(CHUNK):
+                bank = bank_pool.tile([P, HALF], F32, name="bank")
+                for b in range(BATCH):
+                    words = h_raw[c][:, b, :].bitcast(F32)
+                    for u in range(2):
+                        nc.tensor.transpose(
+                            bank[:, (2 * b + u) * P : (2 * b + u + 1) * P],
+                            words[:, WORDS_PASS * i + u : WORDS_PASS * (i + 1) : 2],
+                            ident[:],
+                        )
+                nc.scalar.copy(
+                    out=grouped_words[:, HALF * i : HALF * (i + 1)].rearrange(
+                        "p (b s u) -> p b s u", b=BATCH, u=2
+                    ),
+                    in_=bank[:].rearrange("p (b u s) -> p b s u", b=BATCH, u=2),
+                )
+            return grouped
+
+        def quantise_chunk(c, grouped):
+            cols = slice(c * CHUNK * BATCH * P, (c + 1) * CHUNK * BATCH * P)
+            nc.vector.quantize_mx(
+                out=h_codes[:, cols].bitcast(FP8X4), scales=h_planes[:, cols], in_=grouped[:]
+            )
+
+        def multiply_chunk(c):
+            for i in range(CHUNK):
+                g = CHUNK * c + i
+                for b in range(BATCH):
+                    rows_gb = slice((g * BATCH + b) * P, (g * BATCH + b + 1) * P)
+                    for j in range(HALVES):
+                        n_cols = slice(j * HALF, (j + 1) * HALF)
+                        nc.tensor.matmul_mx(
+                            out=acc[b][j][:],
+                            lhsT=h_codes[:, rows_gb].bitcast(FP8X4),
+                            lhsT_scale=h_planes[:, rows_gb],
+                            rhs=w_sb[g][:, n_cols].bitcast(FP8X4),
+                            rhs_scale=w_planes[4 * i : P, c, n_cols],
+                            start=(g == 0),
+                            stop=(g == PASSES - 1),
+                        )
+
+        def spread_row(v):
+            for j in range(HALVES):
+                n_cols = slice(j * HALF, (j + 1) * HALF)
+                bank = bank_pool.tile([P, HALF], F32, name="bank")
+                nc.tensor.matmul(bank[:], lhsT=ones[:], rhs=rows[:, v, n_cols], start=True, stop=True)
+                nc.scalar.copy(out=spread[:, v, n_cols], in_=bank[:])
+
+        quantise_chunk(0, transpose_chunk(0))
+        for c in range(CHUNKS):
+            if c + 1 < CHUNKS:
+                grouped_next = transpose_chunk(c + 1)
+            if c < 3:
+                spread_row(c)
+            multiply_chunk(c)
+            if c + 1 < CHUNKS:
+                quantise_chunk(c + 1, grouped_next)
+            if c == CHUNKS - 2:
+                for b in range(BATCH):
+                    nc.vector.tensor_tensor(
+                        out=shift_x[:, b, :], in0=spread[:, 2, :], in1=x_sb[:, b, :], op=ALU.add
+                    )
+
+        o = keep.tile([P, BATCH, N], F32)
+        centred = keep.tile([P, BATCH, N], F32)
+        squares = keep.tile([P, N], F32)
+        sums = keep.tile([P, BATCH, HALVES], F32)
+        neg_mean = keep.tile([P, BATCH], F32)
+        sum_sq = keep.tile([P, BATCH], F32)
+        std = keep.tile([P, BATCH], F32)
+        rstd = keep.tile([P, BATCH], F32)
+
+        def add_bias_and_centre(b):
+            for j in range(HALVES):
+                n_cols = slice(j * HALF, (j + 1) * HALF)
+                nc.vector.scalar_tensor_tensor(
+                    out=o[:, b, n_cols], in0=acc[b][j][:], scalar=1.0, in1=spread[:, 0, n_cols],
+                    op0=ALU.mult, op1=ALU.add, accum_out=sums[:, b, j : j + 1],
+                )
+            nc.vector.tensor_scalar(
+                out=neg_mean[:, b : b + 1], in0=sums[:, b, 0:1], scalar1=sums[:, b, 1:2],
+                scalar2=-1.0 / N, op0=ALU.add, op1=ALU.mult,
+            )
+            nc.scalar.activation(
+                out=squares[:], in_=o[:, b, :], func=ACT.Square, bias=neg_mean[:, b : b + 1],
+                scale=1.0, accum_out=sum_sq[:, b : b + 1],
+            )
+            nc.scalar.activation(
+                out=std[:, b : b + 1], in_=sum_sq[:, b : b + 1], func=ACT.Sqrt, bias=eps_col[:],
+                scale=1.0 / N,
+            )
+            nc.vector.scalar_tensor_tensor(
+                out=centred[:, b, :], in0=o[:, b, :], scalar=neg_mean[:, b : b + 1],
+                in1=spread[:, 1, :], op0=ALU.add, op1=ALU.mult,
+            )
+
+        def scale_and_store(b):
+            nc.vector.reciprocal(out=rstd[:, b : b + 1], in_=std[:, b : b + 1])
+            for j in range(HALVES):
+                n_cols = slice(j * HALF, (j + 1) * HALF)
+                nc.vector.scalar_tensor_tensor(
+                    out=centred[:, b, n_cols], in0=centred[:, b, n_cols], scalar=rstd[:, b : b + 1],
+                    in1=shift_x[:, b, n_cols], op0=ALU.mult, op1=ALU.add,
+                )
+                nc.sync.dma_start(out=out[b, :, n_cols], in_=centred[:, b, n_cols])
+
+        add_bias_and_centre(0)
+        add_bias_and_centre(1)
+        scale_and_store(0)
+        scale_and_store(1)

@@ -23,7 +23,6 @@ HALF = 512
 HALVES = N // HALF
 CHUNK = 4
 CHUNKS = PASSES // CHUNK
-WORDS_PASS = K_PASS // 2
 QUADRANTS = 4
 EPS = 1e-5
 
@@ -36,7 +35,8 @@ def tile_dcadecoderblock_pb_k_kernel(
     nc = tc.nc
     with ExitStack() as ctx:
         keep = ctx.enter_context(tc.tile_pool(name="keep", bufs=1))
-        h_pool = ctx.enter_context(tc.tile_pool(name="h_pool", bufs=3))
+        h_pool = ctx.enter_context(tc.tile_pool(name="h_pool", bufs=2))
+        sorted_pool = ctx.enter_context(tc.tile_pool(name="sorted_pool", bufs=2))
         grouped_pool = ctx.enter_context(tc.tile_pool(name="grouped_pool", bufs=2))
         w_pool = ctx.enter_context(tc.tile_pool(name="w_pool", bufs=5 * CHUNK))
         acc_pool = ctx.enter_context(tc.psum_pool(name="acc_pool", bufs=1))
@@ -102,17 +102,26 @@ def tile_dcadecoderblock_pb_k_kernel(
             for b in range(BATCH)
         ]
 
+        h_sorted = []
+
+        def sort_chunk(c):
+            by_parity = sorted_pool.tile([P, BATCH, CHUNK, 2, P], F32, name="by_parity")
+            nc.vector.tensor_copy(
+                out=by_parity[:],
+                in_=h_raw[c][:].bitcast(F32).rearrange("p b (i w u) -> p b i u w", i=CHUNK, u=2),
+            )
+            h_sorted.append(by_parity)
+
         def transpose_chunk(c):
             grouped = grouped_pool.tile([P, CHUNK * BATCH * P * PACK], BF16, name="grouped", align_bytes=64)
             grouped_words = grouped[:].bitcast(F32)
             for i in range(CHUNK):
                 bank = bank_pool.tile([P, HALF], F32, name="bank")
                 for b in range(BATCH):
-                    words = h_raw[c][:, b, :].bitcast(F32)
                     for u in range(2):
                         nc.tensor.transpose(
                             bank[:, (2 * b + u) * P : (2 * b + u + 1) * P],
-                            words[:, WORDS_PASS * i + u : WORDS_PASS * (i + 1) : 2],
+                            h_sorted[c][:, b, i, u, :],
                             ident[:],
                         )
                 nc.scalar.copy(
@@ -153,6 +162,8 @@ def tile_dcadecoderblock_pb_k_kernel(
                 nc.tensor.matmul(bank[:], lhsT=ones[:], rhs=rows[:, v, n_cols], start=True, stop=True)
                 nc.scalar.copy(out=spread[:, v, n_cols], in_=bank[:])
 
+        sort_chunk(0)
+        sort_chunk(1)
         quantise_chunk(0, transpose_chunk(0))
         for c in range(CHUNKS):
             if c + 1 < CHUNKS:
@@ -160,6 +171,8 @@ def tile_dcadecoderblock_pb_k_kernel(
             if c < 3:
                 spread_row(c)
             multiply_chunk(c)
+            if c + 2 < CHUNKS:
+                sort_chunk(c + 2)
             if c + 1 < CHUNKS:
                 quantise_chunk(c + 1, grouped_next)
             if c == CHUNKS - 2:

@@ -76,9 +76,9 @@ def tile_dcadecoderblock_pb_k_kernel(
 
         def load_w(c):
             for q in range(QUADRANTS):
-                nc.sync.dma_start(
-                    out=w_planes[32 * q : 32 * q + 4 * CHUNK, c, :].bitcast(I32),
-                    in_=w_scales[CHUNK * c : CHUNK * (c + 1), 4 * q : 4 * q + 4, :].bitcast(I32),
+                nc.gpsimd.dma_start(
+                    out=w_planes[32 * q : 32 * q + 4 * CHUNK, c, :].bitcast(F32),
+                    in_=w_scales[CHUNK * c : CHUNK * (c + 1), 4 * q : 4 * q + 4, :].bitcast(F32),
                 )
             for g in range(CHUNK * c, CHUNK * (c + 1)):
                 words = w_pool.tile([P, N], U32, name="words", align_bytes=64)

@@ -24,6 +24,7 @@ HALVES = N // HALF
 CHUNK = 4
 CHUNKS = PASSES // CHUNK
 QUADRANTS = 4
+H_AHEAD = 3
 EPS = 1e-5
 
 FLOPS = 2 * BATCH * P * K * N
@@ -35,10 +36,10 @@ def tile_dcadecoderblock_pb_k_kernel(
     nc = tc.nc
     with ExitStack() as ctx:
         keep = ctx.enter_context(tc.tile_pool(name="keep", bufs=1))
-        h_pool = ctx.enter_context(tc.tile_pool(name="h_pool", bufs=2))
+        h_pool = ctx.enter_context(tc.tile_pool(name="h_pool", bufs=H_AHEAD))
         sorted_pool = ctx.enter_context(tc.tile_pool(name="sorted_pool", bufs=2))
         grouped_pool = ctx.enter_context(tc.tile_pool(name="grouped_pool", bufs=2))
-        w_pool = ctx.enter_context(tc.tile_pool(name="w_pool", bufs=5 * CHUNK))
+        w_pool = ctx.enter_context(tc.tile_pool(name="w_pool", bufs=4 * CHUNK))
         acc_pool = ctx.enter_context(tc.psum_pool(name="acc_pool", bufs=1))
         bank_pool = ctx.enter_context(tc.psum_pool(name="bank_pool", bufs=4))
         ctx.enter_context(tc.manual_schedule())
@@ -88,13 +89,13 @@ def tile_dcadecoderblock_pb_k_kernel(
                 )
                 w_sb.append(words)
 
-        load_h(0)
-        load_h(1)
+        for c in range(H_AHEAD):
+            load_h(c)
         for c in range(CHUNKS):
             load_w(c)
-            if c + 2 < CHUNKS:
-                load_h(c + 2)
-            if c == CHUNKS // 2:
+            if c + H_AHEAD < CHUNKS:
+                load_h(c + H_AHEAD)
+            if c == CHUNKS - 2:
                 nc.sync.dma_start(out=x_sb[:], in_=x.rearrange("b s n -> s b n"))
 
         acc = [

@@ -24,6 +24,7 @@ HALVES = N // HALF
 CHUNK = 4
 CHUNKS = PASSES // CHUNK
 QUADRANTS = 4
+PER_TILE = 8
 H_AHEAD = 3
 EPS = 1e-5
 
@@ -50,20 +51,31 @@ def tile_dcadecoderblock_pb_k_kernel(
         spread = keep.tile([P, 3, N], F32)
         x_sb = keep.tile([P, BATCH, N], BF16)
         shift_x = keep.tile([P, BATCH, N], F32)
-        w_planes = keep.tile([P, CHUNKS, N], U8, align_bytes=64)
         h_codes = keep.tile([P, PASSES * BATCH * P], U32, align_bytes=64)
         h_planes = keep.tile([P, PASSES * BATCH * P], U8, align_bytes=64)
         eps_col = keep.tile([P, 1], F32)
         warm = keep.tile([P, 1], F32)
+        sums = keep.tile([P, BATCH, HALVES], F32)
+        pivot = keep.tile([P, BATCH], F32)
+        squares = keep.tile([P, HALF], BF16)
+        sum_sq = keep.tile([P, BATCH, HALVES], F32)
+        var_part = keep.tile([P, BATCH, HALVES], F32)
+        neg_mean = keep.tile([P, BATCH], F32)
+        gap_sq = keep.tile([P, BATCH], F32)
+        rstd = keep.tile([P, BATCH], F32)
 
-        nc.vector.memset(w_planes[:].rearrange("p c n -> p (c n)").bitcast(I32), 0)
-        nc.vector.memset(rows[:], 0.0)
-        nc.vector.memset(ones[:], 1.0)
+        w_planes = [
+            keep.tile([P, PER_TILE, N], U8, name="planes%d" % i, align_bytes=64)
+            for i in range(PASSES // PER_TILE)
+        ]
+
+        def zero_planes(engine, i):
+            engine.memset(w_planes[i][:].rearrange("p e n -> p (e n)").bitcast(I32), 0)
+
+        zero_planes(nc.vector, 0)
         nc.vector.memset(eps_col[:], EPS)
         make_identity(nc, ident[:])
-        for v, vec in enumerate((proj_bias, norm_gain, norm_shift)):
-            nc.scalar.dma_start(out=rows[0:1, v, :], in_=vec.unsqueeze(0))
-        nc.scalar.activation(out=warm[:], in_=eps_col[:], func=ACT.Sqrt)
+        nc.scalar.activation(out=warm[:], in_=eps_col[:], func=ACT.Abs_reciprocal_sqrt)
 
         h_view = h_attn.rearrange("b s k -> s b k")
         h_raw = []
@@ -75,21 +87,38 @@ def tile_dcadecoderblock_pb_k_kernel(
             nc.sync.dma_start(out=raw[:], in_=h_view[:, :, k_cols])
             h_raw.append(raw)
 
-        def load_w(c):
+        def load_scales(i):
+            queue, words = (nc.sync, I32) if i == 0 else (nc.gpsimd, F32)
             for q in range(QUADRANTS):
-                nc.gpsimd.dma_start(
-                    out=w_planes[32 * q : 32 * q + 4 * CHUNK, c, :].bitcast(F32),
-                    in_=w_scales[CHUNK * c : CHUNK * (c + 1), 4 * q : 4 * q + 4, :].bitcast(F32),
+                queue.dma_start(
+                    out=w_planes[i][32 * q : 32 * q + 4, :, :].bitcast(words),
+                    in_=w_scales[PER_TILE * i : PER_TILE * (i + 1), 4 * q : 4 * q + 4, :]
+                    .rearrange("e r n -> r e n").bitcast(words),
                 )
-            for g in range(CHUNK * c, CHUNK * (c + 1)):
-                words = w_pool.tile([P, N], U32, name="words", align_bytes=64)
-                nc.sync.dma_start(
-                    out=words[:].bitcast(I32),
-                    in_=w_words[g].rearrange("p n t -> p (n t)").bitcast(I32),
-                )
-                w_sb.append(words)
 
-        for c in range(H_AHEAD):
+        def load_w(c):
+            pieces = [slice(0, N)]
+            if c == CHUNKS - 1:
+                pieces = [slice(j * HALF, (j + 1) * HALF) for j in range(HALVES)]
+            passes = range(CHUNK * c, CHUNK * (c + 1))
+            for g in passes:
+                w_sb.append(w_pool.tile([P, N], U32, name="words", align_bytes=64))
+            for n_cols in pieces:
+                for g in passes:
+                    nc.sync.dma_start(
+                        out=w_sb[g][:, n_cols].bitcast(I32),
+                        in_=w_words[g][:, n_cols, :].rearrange("p n t -> p (n t)").bitcast(I32),
+                    )
+
+        load_h(0)
+        load_scales(0)
+        for i in range(1, PASSES // PER_TILE):
+            zero_planes(nc.gpsimd, i)
+            load_scales(i)
+        nc.gpsimd.memset(rows[:].rearrange("p v n -> p (v n)").bitcast(I32), 0)
+        for v, vec in enumerate((proj_bias, norm_gain, norm_shift)):
+            nc.gpsimd.dma_start(out=rows[0:1, v, :], in_=vec.unsqueeze(0))
+        for c in range(1, H_AHEAD):
             load_h(c)
         for c in range(CHUNKS):
             load_w(c)
@@ -139,22 +168,23 @@ def tile_dcadecoderblock_pb_k_kernel(
                 out=h_codes[:, cols].bitcast(FP8X4), scales=h_planes[:, cols], in_=grouped[:]
             )
 
-        def multiply_chunk(c):
-            for i in range(CHUNK):
-                g = CHUNK * c + i
-                for b in range(BATCH):
-                    rows_gb = slice((g * BATCH + b) * P, (g * BATCH + b + 1) * P)
-                    for j in range(HALVES):
-                        n_cols = slice(j * HALF, (j + 1) * HALF)
-                        nc.tensor.matmul_mx(
-                            out=acc[b][j][:],
-                            lhsT=h_codes[:, rows_gb].bitcast(FP8X4),
-                            lhsT_scale=h_planes[:, rows_gb],
-                            rhs=w_sb[g][:, n_cols].bitcast(FP8X4),
-                            rhs_scale=w_planes[4 * i : P, c, n_cols],
-                            start=(g == 0),
-                            stop=(g == PASSES - 1),
-                        )
+        def multiply(g, b, j):
+            rows_gb = slice((g * BATCH + b) * P, (g * BATCH + b + 1) * P)
+            n_cols = slice(j * HALF, (j + 1) * HALF)
+            nc.tensor.matmul_mx(
+                out=acc[b][j][:],
+                lhsT=h_codes[:, rows_gb].bitcast(FP8X4),
+                lhsT_scale=h_planes[:, rows_gb],
+                rhs=w_sb[g][:, n_cols].bitcast(FP8X4),
+                rhs_scale=w_planes[g // PER_TILE][:, g % PER_TILE, n_cols],
+                start=(g == 0),
+                stop=(g == PASSES - 1),
+            )
+
+        def multiply_chunk(c, sums_of):
+            for g in range(CHUNK * c, CHUNK * (c + 1)):
+                for b, j in sums_of:
+                    multiply(g, b, j)
 
         def spread_row(v):
             for j in range(HALVES):
@@ -163,60 +193,45 @@ def tile_dcadecoderblock_pb_k_kernel(
                 nc.tensor.matmul(bank[:], lhsT=ones[:], rhs=rows[:, v, n_cols], start=True, stop=True)
                 nc.scalar.copy(out=spread[:, v, n_cols], in_=bank[:])
 
-        sort_chunk(0)
-        sort_chunk(1)
-        quantise_chunk(0, transpose_chunk(0))
-        for c in range(CHUNKS):
-            if c + 1 < CHUNKS:
-                grouped_next = transpose_chunk(c + 1)
-            if c < 3:
-                spread_row(c)
-            multiply_chunk(c)
-            if c + 2 < CHUNKS:
-                sort_chunk(c + 2)
-            if c + 1 < CHUNKS:
-                quantise_chunk(c + 1, grouped_next)
-            if c == CHUNKS - 2:
-                for b in range(BATCH):
-                    nc.vector.tensor_tensor(
-                        out=shift_x[:, b, :], in0=spread[:, 2, :], in1=x_sb[:, b, :], op=ALU.add
-                    )
-
-        o = keep.tile([P, BATCH, N], F32)
-        centred = keep.tile([P, BATCH, N], F32)
-        squares = keep.tile([P, N], F32)
-        sums = keep.tile([P, BATCH, HALVES], F32)
-        neg_mean = keep.tile([P, BATCH], F32)
-        sum_sq = keep.tile([P, BATCH], F32)
-        std = keep.tile([P, BATCH], F32)
-        rstd = keep.tile([P, BATCH], F32)
-
-        def add_bias_and_centre(b):
-            for j in range(HALVES):
-                n_cols = slice(j * HALF, (j + 1) * HALF)
-                nc.vector.scalar_tensor_tensor(
-                    out=o[:, b, n_cols], in0=acc[b][j][:], scalar=1.0, in1=spread[:, 0, n_cols],
-                    op0=ALU.mult, op1=ALU.add, accum_out=sums[:, b, j : j + 1],
+        def add_bias(b, j):
+            n_cols = slice(j * HALF, (j + 1) * HALF)
+            nc.vector.scalar_tensor_tensor(
+                out=o[:, b, n_cols], in0=acc[b][j][:], scalar=1.0, in1=spread[:, 0, n_cols],
+                op0=ALU.mult, op1=ALU.add, accum_out=sums[:, b, j : j + 1],
+            )
+            if j == 0:
+                nc.vector.tensor_scalar_mul(
+                    out=pivot[:, b : b + 1], in0=sums[:, b, 0:1], scalar1=1.0 / HALF
                 )
+
+        def add_squares(b, j):
+            n_cols = slice(j * HALF, (j + 1) * HALF)
+            nc.scalar.activation(
+                out=squares[:], in_=o[:, b, n_cols], func=ACT.Square, bias=pivot[:, b : b + 1],
+                scale=-1.0, accum_out=sum_sq[:, b, j : j + 1],
+            )
+            nc.scalar.activation(
+                out=var_part[:, b, j : j + 1], in_=sum_sq[:, b, j : j + 1], func=ACT.Identity,
+                bias=eps_col[:] if j == 0 else var_part[:, b, 0:1], scale=1.0 / N,
+            )
+
+        def finish(b):
             nc.vector.tensor_scalar(
                 out=neg_mean[:, b : b + 1], in0=sums[:, b, 0:1], scalar1=sums[:, b, 1:2],
                 scalar2=-1.0 / N, op0=ALU.add, op1=ALU.mult,
-            )
-            nc.scalar.activation(
-                out=squares[:], in_=o[:, b, :], func=ACT.Square, bias=neg_mean[:, b : b + 1],
-                scale=1.0, accum_out=sum_sq[:, b : b + 1],
-            )
-            nc.scalar.activation(
-                out=std[:, b : b + 1], in_=sum_sq[:, b : b + 1], func=ACT.Sqrt, bias=eps_col[:],
-                scale=1.0 / N,
             )
             nc.vector.scalar_tensor_tensor(
                 out=centred[:, b, :], in0=o[:, b, :], scalar=neg_mean[:, b : b + 1],
                 in1=spread[:, 1, :], op0=ALU.add, op1=ALU.mult,
             )
-
-        def scale_and_store(b):
-            nc.vector.reciprocal(out=rstd[:, b : b + 1], in_=std[:, b : b + 1])
+            nc.scalar.activation(
+                out=gap_sq[:, b : b + 1], in_=neg_mean[:, b : b + 1], func=ACT.Square,
+                bias=pivot[:, b : b + 1], scale=1.0,
+            )
+            nc.scalar.activation(
+                out=rstd[:, b : b + 1], in_=gap_sq[:, b : b + 1], func=ACT.Abs_reciprocal_sqrt,
+                bias=var_part[:, b, 1:2], scale=-1.0,
+            )
             for j in range(HALVES):
                 n_cols = slice(j * HALF, (j + 1) * HALF)
                 nc.vector.scalar_tensor_tensor(
@@ -225,7 +240,37 @@ def tile_dcadecoderblock_pb_k_kernel(
                 )
                 nc.sync.dma_start(out=out[b, :, n_cols], in_=centred[:, b, n_cols])
 
-        add_bias_and_centre(0)
-        add_bias_and_centre(1)
-        scale_and_store(0)
-        scale_and_store(1)
+        last = CHUNKS - 1
+        all_sums = [(b, j) for b in range(BATCH) for j in range(HALVES)]
+        sort_chunk(0)
+        sort_chunk(1)
+        quantise_chunk(0, transpose_chunk(0))
+        nc.vector.memset(ones[:], 1.0)
+        for c in range(last):
+            grouped_next = transpose_chunk(c + 1)
+            if c == last - 2:
+                spread_row(0)
+                spread_row(1)
+            if c == last - 1:
+                spread_row(2)
+            multiply_chunk(c, all_sums if c < last - 1 else all_sums[:-1])
+            if c + 2 < CHUNKS:
+                sort_chunk(c + 2)
+            quantise_chunk(c + 1, grouped_next)
+        for b in range(BATCH):
+            nc.vector.tensor_tensor(
+                out=shift_x[:, b, :], in0=spread[:, 2, :], in1=x_sb[:, b, :], op=ALU.add
+            )
+        o = sorted_pool.tile([P, BATCH, N], F32, name="by_parity")
+        centred = sorted_pool.tile([P, BATCH, N], F32, name="by_parity")
+        multiply_chunk(last, [(0, 0), (1, 0)])
+        for b in range(BATCH):
+            add_bias(b, 0)
+            add_squares(b, 0)
+        multiply_chunk(last, [(0, 1)])
+        for c in (last - 1, last):
+            multiply_chunk(c, [(1, 1)])
+        for b in range(BATCH):
+            add_bias(b, 1)
+            add_squares(b, 1)
+            finish(b)

@@ -24,7 +24,6 @@ HALVES = N // HALF
 CHUNK = 4
 CHUNKS = PASSES // CHUNK
 QUADRANTS = 4
-PER_TILE = 8
 H_AHEAD = 3
 EPS = 1e-5
 
@@ -64,15 +63,8 @@ def tile_dcadecoderblock_pb_k_kernel(
         gap_sq = keep.tile([P, BATCH], F32)
         rstd = keep.tile([P, BATCH], F32)
 
-        w_planes = [
-            keep.tile([P, PER_TILE, N], U8, name="planes%d" % i, align_bytes=64)
-            for i in range(PASSES // PER_TILE)
-        ]
-
-        def zero_planes(engine, i):
-            engine.memset(w_planes[i][:].rearrange("p e n -> p (e n)").bitcast(I32), 0)
-
-        zero_planes(nc.vector, 0)
+        w_planes = keep.tile([P, CHUNKS, N], U8, align_bytes=64)
+        nc.vector.memset(w_planes[:].rearrange("p c n -> p (c n)").bitcast(I32), 0)
         nc.vector.memset(eps_col[:], EPS)
         make_identity(nc, ident[:])
         nc.scalar.activation(out=warm[:], in_=eps_col[:], func=ACT.Abs_reciprocal_sqrt)
@@ -87,13 +79,11 @@ def tile_dcadecoderblock_pb_k_kernel(
             nc.sync.dma_start(out=raw[:], in_=h_view[:, :, k_cols])
             h_raw.append(raw)
 
-        def load_scales(i):
-            queue, words = (nc.sync, I32) if i == 0 else (nc.gpsimd, F32)
+        def load_scales(c):
             for q in range(QUADRANTS):
-                queue.dma_start(
-                    out=w_planes[i][32 * q : 32 * q + 4, :, :].bitcast(words),
-                    in_=w_scales[PER_TILE * i : PER_TILE * (i + 1), 4 * q : 4 * q + 4, :]
-                    .rearrange("e r n -> r e n").bitcast(words),
+                nc.gpsimd.dma_start(
+                    out=w_planes[32 * q : 32 * q + 4 * CHUNK, c, :].bitcast(F32),
+                    in_=w_scales[CHUNK * c : CHUNK * (c + 1), 4 * q : 4 * q + 4, :].bitcast(F32),
                 )
 
         def load_w(c):
@@ -110,17 +100,10 @@ def tile_dcadecoderblock_pb_k_kernel(
                         in_=w_words[g][:, n_cols, :].rearrange("p n t -> p (n t)").bitcast(I32),
                     )
 
-        load_h(0)
-        load_scales(0)
-        for i in range(1, PASSES // PER_TILE):
-            zero_planes(nc.gpsimd, i)
-            load_scales(i)
-        nc.gpsimd.memset(rows[:].rearrange("p v n -> p (v n)").bitcast(I32), 0)
-        for v, vec in enumerate((proj_bias, norm_gain, norm_shift)):
-            nc.gpsimd.dma_start(out=rows[0:1, v, :], in_=vec.unsqueeze(0))
-        for c in range(1, H_AHEAD):
+        for c in range(H_AHEAD):
             load_h(c)
         for c in range(CHUNKS):
+            load_scales(c)
             load_w(c)
             if c + H_AHEAD < CHUNKS:
                 load_h(c + H_AHEAD)
@@ -176,7 +159,7 @@ def tile_dcadecoderblock_pb_k_kernel(
                 lhsT=h_codes[:, rows_gb].bitcast(FP8X4),
                 lhsT_scale=h_planes[:, rows_gb],
                 rhs=w_sb[g][:, n_cols].bitcast(FP8X4),
-                rhs_scale=w_planes[g // PER_TILE][:, g % PER_TILE, n_cols],
+                rhs_scale=w_planes[4 * (g % CHUNK) : P, g // CHUNK, n_cols],
                 start=(g == 0),
                 stop=(g == PASSES - 1),
             )
@@ -245,7 +228,10 @@ def tile_dcadecoderblock_pb_k_kernel(
         sort_chunk(0)
         sort_chunk(1)
         quantise_chunk(0, transpose_chunk(0))
+        nc.vector.memset(rows[:].rearrange("p v n -> p (v n)").bitcast(I32), 0)
         nc.vector.memset(ones[:], 1.0)
+        for v, vec in enumerate((proj_bias, norm_gain, norm_shift)):
+            nc.gpsimd.dma_start(out=rows[0:1, v, :], in_=vec.unsqueeze(0))
         for c in range(last):
             grouped_next = transpose_chunk(c + 1)
             if c == last - 2:

@@ -25,6 +25,7 @@ CHUNK = 4
 CHUNKS = PASSES // CHUNK
 QUADRANTS = 4
 H_AHEAD = 3
+SYNC_SCALES = 2
 EPS = 1e-5
 
 FLOPS = 2 * BATCH * P * K * N
@@ -80,10 +81,11 @@ def tile_dcadecoderblock_pb_k_kernel(
             h_raw.append(raw)
 
         def load_scales(c):
+            queue, words = (nc.sync, I32) if c < SYNC_SCALES else (nc.gpsimd, F32)
             for q in range(QUADRANTS):
-                nc.gpsimd.dma_start(
-                    out=w_planes[32 * q : 32 * q + 4 * CHUNK, c, :].bitcast(F32),
-                    in_=w_scales[CHUNK * c : CHUNK * (c + 1), 4 * q : 4 * q + 4, :].bitcast(F32),
+                queue.dma_start(
+                    out=w_planes[32 * q : 32 * q + 4 * CHUNK, c, :].bitcast(words),
+                    in_=w_scales[CHUNK * c : CHUNK * (c + 1), 4 * q : 4 * q + 4, :].bitcast(words),
                 )
 
         def load_w(c):
@@ -100,10 +102,12 @@ def tile_dcadecoderblock_pb_k_kernel(
                         in_=w_words[g][:, n_cols, :].rearrange("p n t -> p (n t)").bitcast(I32),
                     )
 
-        for c in range(H_AHEAD):
-            load_h(c)
+        load_h(0)
         for c in range(CHUNKS):
             load_scales(c)
+        for c in range(1, H_AHEAD):
+            load_h(c)
+        for c in range(CHUNKS):
             load_w(c)
             if c + H_AHEAD < CHUNKS:
                 load_h(c + H_AHEAD)
@@ -230,10 +234,11 @@ def tile_dcadecoderblock_pb_k_kernel(
         quantise_chunk(0, transpose_chunk(0))
         nc.vector.memset(rows[:].rearrange("p v n -> p (v n)").bitcast(I32), 0)
         nc.vector.memset(ones[:], 1.0)
-        for v, vec in enumerate((proj_bias, norm_gain, norm_shift)):
-            nc.gpsimd.dma_start(out=rows[0:1, v, :], in_=vec.unsqueeze(0))
         for c in range(last):
             grouped_next = transpose_chunk(c + 1)
+            if c == 2:
+                for v, vec in enumerate((proj_bias, norm_gain, norm_shift)):
+                    nc.scalar.dma_start(out=rows[0:1, v, :], in_=vec.unsqueeze(0))
             if c == last - 2:
                 spread_row(0)
                 spread_row(1)

@@ -23,9 +23,10 @@ HALF = 512
 HALVES = N // HALF
 CHUNK = 4
 CHUNKS = PASSES // CHUNK
+RUN = 2
 QUADRANTS = 4
 H_AHEAD = 3
-SYNC_SCALES = 2
+SYNC_SCALES = 1
 EPS = 1e-5
 
 FLOPS = 2 * BATCH * P * K * N
@@ -40,7 +41,7 @@ def tile_dcadecoderblock_pb_k_kernel(
         h_pool = ctx.enter_context(tc.tile_pool(name="h_pool", bufs=H_AHEAD))
         sorted_pool = ctx.enter_context(tc.tile_pool(name="sorted_pool", bufs=2))
         grouped_pool = ctx.enter_context(tc.tile_pool(name="grouped_pool", bufs=2))
-        w_pool = ctx.enter_context(tc.tile_pool(name="w_pool", bufs=4 * CHUNK))
+        w_pool = ctx.enter_context(tc.tile_pool(name="w_pool", bufs=4 * CHUNK // RUN))
         acc_pool = ctx.enter_context(tc.psum_pool(name="acc_pool", bufs=1))
         bank_pool = ctx.enter_context(tc.psum_pool(name="bank_pool", bufs=4))
         ctx.enter_context(tc.manual_schedule())
@@ -51,8 +52,8 @@ def tile_dcadecoderblock_pb_k_kernel(
         spread = keep.tile([P, 3, N], F32)
         x_sb = keep.tile([P, BATCH, N], BF16)
         shift_x = keep.tile([P, BATCH, N], F32)
-        h_codes = keep.tile([P, PASSES * BATCH * P], U32, align_bytes=64)
-        h_planes = keep.tile([P, PASSES * BATCH * P], U8, align_bytes=64)
+        h_codes = keep.tile([P, PASSES * BATCH * P], U32, align_bytes=256)
+        h_planes = keep.tile([P, PASSES * BATCH * P], U8, align_bytes=256)
         eps_col = keep.tile([P, 1], F32)
         warm = keep.tile([P, 1], F32)
         sums = keep.tile([P, BATCH, HALVES], F32)
@@ -64,10 +65,14 @@ def tile_dcadecoderblock_pb_k_kernel(
         gap_sq = keep.tile([P, BATCH], F32)
         rstd = keep.tile([P, BATCH], F32)
 
-        w_planes = keep.tile([P, CHUNKS, N], U8, align_bytes=64)
-        nc.vector.memset(w_planes[:].rearrange("p c n -> p (c n)").bitcast(I32), 0)
+        w_planes = keep.tile([P, CHUNKS, N], U8, align_bytes=256)
         nc.vector.memset(eps_col[:], EPS)
+        nc.vector.memset(rows[:].rearrange("p v n -> p (v n)").bitcast(I32), 0)
+        nc.vector.memset(w_planes[:].rearrange("p c n -> p (c n)").bitcast(I32), 0)
+        nc.vector.memset(ones[:], 1.0)
         make_identity(nc, ident[:])
+        for v, vec in enumerate((proj_bias, norm_gain, norm_shift)):
+            nc.scalar.dma_start(out=rows[0:1, v, :], in_=vec.unsqueeze(0))
         nc.scalar.activation(out=warm[:], in_=eps_col[:], func=ACT.Abs_reciprocal_sqrt)
 
         h_view = h_attn.rearrange("b s k -> s b k")
@@ -89,18 +94,27 @@ def tile_dcadecoderblock_pb_k_kernel(
                 )
 
         def load_w(c):
-            pieces = [slice(0, N)]
-            if c == CHUNKS - 1:
-                pieces = [slice(j * HALF, (j + 1) * HALF) for j in range(HALVES)]
-            passes = range(CHUNK * c, CHUNK * (c + 1))
-            for g in passes:
-                w_sb.append(w_pool.tile([P, N], U32, name="words", align_bytes=64))
-            for n_cols in pieces:
-                for g in passes:
+            tiles = []
+            for first in range(CHUNK * c, CHUNK * (c + 1), RUN):
+                words = w_pool.tile([P, RUN, N], U32, name="words", align_bytes=256)
+                tiles.append((first, words))
+                for e in range(RUN):
+                    w_sb.append(words[:, e, :])
+            if c < CHUNKS - 1:
+                for g in range(CHUNK * c, CHUNK * (c + 1)):
                     nc.sync.dma_start(
-                        out=w_sb[g][:, n_cols].bitcast(I32),
-                        in_=w_words[g][:, n_cols, :].rearrange("p n t -> p (n t)").bitcast(I32),
+                        out=w_sb[g].bitcast(I32), in_=w_words[g].rearrange("p n t -> p (n t)").bitcast(I32)
                     )
+            else:
+                for j in range(HALVES):
+                    n_cols = slice(j * HALF, (j + 1) * HALF)
+                    for first, words in tiles:
+                        nc.sync.dma_start(
+                            out=words[:, :, n_cols].bitcast(I32),
+                            in_=w_words[first : first + RUN, :, n_cols, :]
+                            .rearrange("g p n t -> p g (n t)")
+                            .bitcast(I32),
+                        )
 
         load_h(0)
         for c in range(CHUNKS):
@@ -111,7 +125,7 @@ def tile_dcadecoderblock_pb_k_kernel(
             load_w(c)
             if c + H_AHEAD < CHUNKS:
                 load_h(c + H_AHEAD)
-            if c == CHUNKS - 2:
+            if c == CHUNKS - 3:
                 nc.sync.dma_start(out=x_sb[:], in_=x.rearrange("b s n -> s b n"))
 
         acc = [
@@ -129,10 +143,12 @@ def tile_dcadecoderblock_pb_k_kernel(
             )
             h_sorted.append(by_parity)
 
-        def transpose_chunk(c):
-            grouped = grouped_pool.tile([P, CHUNK * BATCH * P * PACK], BF16, name="grouped", align_bytes=64)
+        def new_grouped():
+            return grouped_pool.tile([P, CHUNK * BATCH * P * PACK], BF16, name="grouped", align_bytes=64)
+
+        def transpose_run(c, first, grouped):
             grouped_words = grouped[:].bitcast(F32)
-            for i in range(CHUNK):
+            for i in range(first, first + RUN):
                 bank = bank_pool.tile([P, HALF], F32, name="bank")
                 for b in range(BATCH):
                     for u in range(2):
@@ -147,7 +163,6 @@ def tile_dcadecoderblock_pb_k_kernel(
                     ),
                     in_=bank[:].rearrange("p (b u s) -> p b s u", b=BATCH, u=2),
                 )
-            return grouped
 
         def quantise_chunk(c, grouped):
             cols = slice(c * CHUNK * BATCH * P, (c + 1) * CHUNK * BATCH * P)
@@ -168,10 +183,11 @@ def tile_dcadecoderblock_pb_k_kernel(
                 stop=(g == PASSES - 1),
             )
 
-        def multiply_chunk(c, sums_of):
-            for g in range(CHUNK * c, CHUNK * (c + 1)):
-                for b, j in sums_of:
-                    multiply(g, b, j)
+        def multiply_run(first):
+            for g in range(first, first + RUN):
+                for b in range(BATCH):
+                    for j in range(HALVES):
+                        multiply(g, b, j)
 
         def spread_row(v):
             for j in range(HALVES):
@@ -202,14 +218,10 @@ def tile_dcadecoderblock_pb_k_kernel(
                 bias=eps_col[:] if j == 0 else var_part[:, b, 0:1], scale=1.0 / N,
             )
 
-        def finish(b):
+        def add_mean(b):
             nc.vector.tensor_scalar(
                 out=neg_mean[:, b : b + 1], in0=sums[:, b, 0:1], scalar1=sums[:, b, 1:2],
                 scalar2=-1.0 / N, op0=ALU.add, op1=ALU.mult,
-            )
-            nc.vector.scalar_tensor_tensor(
-                out=centred[:, b, :], in0=o[:, b, :], scalar=neg_mean[:, b : b + 1],
-                in1=spread[:, 1, :], op0=ALU.add, op1=ALU.mult,
             )
             nc.scalar.activation(
                 out=gap_sq[:, b : b + 1], in_=neg_mean[:, b : b + 1], func=ACT.Square,
@@ -219,6 +231,14 @@ def tile_dcadecoderblock_pb_k_kernel(
                 out=rstd[:, b : b + 1], in_=gap_sq[:, b : b + 1], func=ACT.Abs_reciprocal_sqrt,
                 bias=var_part[:, b, 1:2], scale=-1.0,
             )
+
+        def centre(b):
+            nc.vector.scalar_tensor_tensor(
+                out=centred[:, b, :], in0=o[:, b, :], scalar=neg_mean[:, b : b + 1],
+                in1=spread[:, 1, :], op0=ALU.add, op1=ALU.mult,
+            )
+
+        def scale_and_store(b):
             for j in range(HALVES):
                 n_cols = slice(j * HALF, (j + 1) * HALF)
                 nc.vector.scalar_tensor_tensor(
@@ -228,40 +248,39 @@ def tile_dcadecoderblock_pb_k_kernel(
                 nc.sync.dma_start(out=out[b, :, n_cols], in_=centred[:, b, n_cols])
 
         last = CHUNKS - 1
-        all_sums = [(b, j) for b in range(BATCH) for j in range(HALVES)]
         sort_chunk(0)
         sort_chunk(1)
-        quantise_chunk(0, transpose_chunk(0))
-        nc.vector.memset(rows[:].rearrange("p v n -> p (v n)").bitcast(I32), 0)
-        nc.vector.memset(ones[:], 1.0)
+        grouped = new_grouped()
+        for first in range(0, CHUNK, RUN):
+            transpose_run(0, first, grouped)
+        quantise_chunk(0, grouped)
+        for v in range(3):
+            spread_row(v)
         for c in range(last):
-            grouped_next = transpose_chunk(c + 1)
-            if c == 2:
-                for v, vec in enumerate((proj_bias, norm_gain, norm_shift)):
-                    nc.scalar.dma_start(out=rows[0:1, v, :], in_=vec.unsqueeze(0))
-            if c == last - 2:
-                spread_row(0)
-                spread_row(1)
-            if c == last - 1:
-                spread_row(2)
-            multiply_chunk(c, all_sums if c < last - 1 else all_sums[:-1])
+            grouped = new_grouped()
+            for first in range(0, CHUNK, RUN):
+                transpose_run(c + 1, first, grouped)
+                multiply_run(CHUNK * c + first)
             if c + 2 < CHUNKS:
                 sort_chunk(c + 2)
-            quantise_chunk(c + 1, grouped_next)
-        for b in range(BATCH):
-            nc.vector.tensor_tensor(
-                out=shift_x[:, b, :], in0=spread[:, 2, :], in1=x_sb[:, b, :], op=ALU.add
-            )
+            quantise_chunk(c + 1, grouped)
+            if c == last - 2:
+                for b in range(BATCH):
+                    nc.vector.tensor_tensor(
+                        out=shift_x[:, b, :], in0=spread[:, 2, :], in1=x_sb[:, b, :], op=ALU.add
+                    )
+
         o = sorted_pool.tile([P, BATCH, N], F32, name="by_parity")
         centred = sorted_pool.tile([P, BATCH, N], F32, name="by_parity")
-        multiply_chunk(last, [(0, 0), (1, 0)])
+        for j in range(HALVES):
+            for b in range(BATCH):
+                for g in range(CHUNK * last, PASSES):
+                    multiply(g, b, j)
+                add_bias(b, j)
+                add_squares(b, j)
+                if j == HALVES - 1:
+                    add_mean(b)
         for b in range(BATCH):
-            add_bias(b, 0)
-            add_squares(b, 0)
-        multiply_chunk(last, [(0, 1)])
-        for c in (last - 1, last):
-            multiply_chunk(c, [(1, 1)])
+            centre(b)
         for b in range(BATCH):
-            add_bias(b, 1)
-            add_squares(b, 1)
-            finish(b)
+            scale_and_store(b)

@@ -23,10 +23,10 @@ HALF = 512
 HALVES = N // HALF
 CHUNK = 4
 CHUNKS = PASSES // CHUNK
-RUN = 2
+PAIR = 2
 QUADRANTS = 4
 H_AHEAD = 3
-SYNC_SCALES = 1
+T_AHEAD = 2
 EPS = 1e-5
 
 FLOPS = 2 * BATCH * P * K * N
@@ -41,7 +41,7 @@ def tile_dcadecoderblock_pb_k_kernel(
         h_pool = ctx.enter_context(tc.tile_pool(name="h_pool", bufs=H_AHEAD))
         sorted_pool = ctx.enter_context(tc.tile_pool(name="sorted_pool", bufs=2))
         grouped_pool = ctx.enter_context(tc.tile_pool(name="grouped_pool", bufs=2))
-        w_pool = ctx.enter_context(tc.tile_pool(name="w_pool", bufs=4 * CHUNK // RUN))
+        w_pool = ctx.enter_context(tc.tile_pool(name="w_pool", bufs=4 * CHUNK // PAIR))
         acc_pool = ctx.enter_context(tc.psum_pool(name="acc_pool", bufs=1))
         bank_pool = ctx.enter_context(tc.psum_pool(name="bank_pool", bufs=4))
         ctx.enter_context(tc.manual_schedule())
@@ -67,8 +67,8 @@ def tile_dcadecoderblock_pb_k_kernel(
 
         w_planes = keep.tile([P, CHUNKS, N], U8, align_bytes=256)
         nc.vector.memset(eps_col[:], EPS)
-        nc.vector.memset(rows[:].rearrange("p v n -> p (v n)").bitcast(I32), 0)
         nc.vector.memset(w_planes[:].rearrange("p c n -> p (c n)").bitcast(I32), 0)
+        nc.vector.memset(rows[:].rearrange("p v n -> p (v n)").bitcast(I32), 0)
         nc.vector.memset(ones[:], 1.0)
         make_identity(nc, ident[:])
         for v, vec in enumerate((proj_bias, norm_gain, norm_shift)):
@@ -86,45 +86,43 @@ def tile_dcadecoderblock_pb_k_kernel(
             h_raw.append(raw)
 
         def load_scales(c):
-            queue, words = (nc.sync, I32) if c < SYNC_SCALES else (nc.gpsimd, F32)
             for q in range(QUADRANTS):
-                queue.dma_start(
-                    out=w_planes[32 * q : 32 * q + 4 * CHUNK, c, :].bitcast(words),
-                    in_=w_scales[CHUNK * c : CHUNK * (c + 1), 4 * q : 4 * q + 4, :].bitcast(words),
+                nc.gpsimd.dma_start(
+                    out=w_planes[32 * q : 32 * q + 4 * CHUNK, c, :].bitcast(F32),
+                    in_=w_scales[CHUNK * c : CHUNK * (c + 1), 4 * q : 4 * q + 4, :].bitcast(F32),
                 )
 
         def load_w(c):
             tiles = []
-            for first in range(CHUNK * c, CHUNK * (c + 1), RUN):
-                words = w_pool.tile([P, RUN, N], U32, name="words", align_bytes=256)
+            for first in range(CHUNK * c, CHUNK * (c + 1), PAIR):
+                words = w_pool.tile([P, PAIR, N], U32, name="words", align_bytes=256)
                 tiles.append((first, words))
-                for e in range(RUN):
+                for e in range(PAIR):
                     w_sb.append(words[:, e, :])
             if c < CHUNKS - 1:
                 for g in range(CHUNK * c, CHUNK * (c + 1)):
                     nc.sync.dma_start(
                         out=w_sb[g].bitcast(I32), in_=w_words[g].rearrange("p n t -> p (n t)").bitcast(I32)
                     )
+                    if g == CHUNK * c and c + H_AHEAD < CHUNKS:
+                        load_h(c + H_AHEAD)
             else:
                 for j in range(HALVES):
                     n_cols = slice(j * HALF, (j + 1) * HALF)
                     for first, words in tiles:
                         nc.sync.dma_start(
                             out=words[:, :, n_cols].bitcast(I32),
-                            in_=w_words[first : first + RUN, :, n_cols, :]
+                            in_=w_words[first : first + PAIR, :, n_cols, :]
                             .rearrange("g p n t -> p g (n t)")
                             .bitcast(I32),
                         )
 
-        load_h(0)
         for c in range(CHUNKS):
             load_scales(c)
-        for c in range(1, H_AHEAD):
+        for c in range(H_AHEAD):
             load_h(c)
         for c in range(CHUNKS):
             load_w(c)
-            if c + H_AHEAD < CHUNKS:
-                load_h(c + H_AHEAD)
             if c == CHUNKS - 3:
                 nc.sync.dma_start(out=x_sb[:], in_=x.rearrange("b s n -> s b n"))
 
@@ -143,12 +141,10 @@ def tile_dcadecoderblock_pb_k_kernel(
             )
             h_sorted.append(by_parity)
 
-        def new_grouped():
-            return grouped_pool.tile([P, CHUNK * BATCH * P * PACK], BF16, name="grouped", align_bytes=64)
-
-        def transpose_run(c, first, grouped):
+        def transpose_chunk(c):
+            grouped = grouped_pool.tile([P, CHUNK * BATCH * P * PACK], BF16, name="grouped", align_bytes=64)
             grouped_words = grouped[:].bitcast(F32)
-            for i in range(first, first + RUN):
+            for i in range(CHUNK):
                 bank = bank_pool.tile([P, HALF], F32, name="bank")
                 for b in range(BATCH):
                     for u in range(2):
@@ -163,6 +159,7 @@ def tile_dcadecoderblock_pb_k_kernel(
                     ),
                     in_=bank[:].rearrange("p (b u s) -> p b s u", b=BATCH, u=2),
                 )
+            return grouped
 
         def quantise_chunk(c, grouped):
             cols = slice(c * CHUNK * BATCH * P, (c + 1) * CHUNK * BATCH * P)
@@ -183,8 +180,8 @@ def tile_dcadecoderblock_pb_k_kernel(
                 stop=(g == PASSES - 1),
             )
 
-        def multiply_run(first):
-            for g in range(first, first + RUN):
+        def multiply_chunk(c):
+            for g in range(CHUNK * c, CHUNK * (c + 1)):
                 for b in range(BATCH):
                     for j in range(HALVES):
                         multiply(g, b, j)
@@ -247,28 +244,26 @@ def tile_dcadecoderblock_pb_k_kernel(
                 )
                 nc.sync.dma_start(out=out[b, :, n_cols], in_=centred[:, b, n_cols])
 
+        def prepare_chunk(c):
+            grouped = transpose_chunk(c)
+            if c + 1 < CHUNKS:
+                sort_chunk(c + 1)
+            quantise_chunk(c, grouped)
+
         last = CHUNKS - 1
         sort_chunk(0)
-        sort_chunk(1)
-        grouped = new_grouped()
-        for first in range(0, CHUNK, RUN):
-            transpose_run(0, first, grouped)
-        quantise_chunk(0, grouped)
+        for c in range(T_AHEAD):
+            prepare_chunk(c)
         for v in range(3):
             spread_row(v)
         for c in range(last):
-            grouped = new_grouped()
-            for first in range(0, CHUNK, RUN):
-                transpose_run(c + 1, first, grouped)
-                multiply_run(CHUNK * c + first)
-            if c + 2 < CHUNKS:
-                sort_chunk(c + 2)
-            quantise_chunk(c + 1, grouped)
-            if c == last - 2:
-                for b in range(BATCH):
-                    nc.vector.tensor_tensor(
-                        out=shift_x[:, b, :], in0=spread[:, 2, :], in1=x_sb[:, b, :], op=ALU.add
-                    )
+            if c + T_AHEAD < CHUNKS:
+                prepare_chunk(c + T_AHEAD)
+            multiply_chunk(c)
+        for b in range(BATCH):
+            nc.vector.tensor_tensor(
+                out=shift_x[:, b, :], in0=spread[:, 2, :], in1=x_sb[:, b, :], op=ALU.add
+            )
 
         o = sorted_pool.tile([P, BATCH, N], F32, name="by_parity")
         centred = sorted_pool.tile([P, BATCH, N], F32, name="by_parity")

from contextlib import ExitStack

import concourse.mybir as mybir
from concourse.masks import make_identity

FP8X4 = mybir.dt.float8_e4m3fn_x4
BF16 = mybir.dt.bfloat16
F32 = mybir.dt.float32
I32 = mybir.dt.int32
U32 = mybir.dt.uint32
U8 = mybir.dt.uint8
ALU = mybir.AluOpType
ACT = mybir.ActivationFunctionType

P = 128
BATCH = 2
K = 16384
N = 1024
PACK = 4
K_PASS = P * PACK
PASSES = K // K_PASS
HALF = 512
HALVES = N // HALF
CHUNK = 4
CHUNKS = PASSES // CHUNK
PAIR = 2
QUADRANTS = 4
H_AHEAD = 3
T_AHEAD = 2
EPS = 1e-5

FLOPS = 2 * BATCH * P * K * N


def tile_dcadecoderblock_pb_k_kernel(
    tc, h_attn, x, w_words, w_scales, proj_bias, norm_gain, norm_shift, out
):
    nc = tc.nc
    with ExitStack() as ctx:
        keep = ctx.enter_context(tc.tile_pool(name="keep", bufs=1))
        h_pool = ctx.enter_context(tc.tile_pool(name="h_pool", bufs=H_AHEAD))
        sorted_pool = ctx.enter_context(tc.tile_pool(name="sorted_pool", bufs=2))
        grouped_pool = ctx.enter_context(tc.tile_pool(name="grouped_pool", bufs=2))
        w_pool = ctx.enter_context(tc.tile_pool(name="w_pool", bufs=4 * CHUNK // PAIR))
        acc_pool = ctx.enter_context(tc.psum_pool(name="acc_pool", bufs=1))
        bank_pool = ctx.enter_context(tc.psum_pool(name="bank_pool", bufs=4))
        ctx.enter_context(tc.manual_schedule())

        ident = keep.tile([P, P], F32)
        ones = keep.tile([P, P], BF16)
        rows = keep.tile([P, 3, N], BF16)
        spread = keep.tile([P, 3, N], F32)
        x_sb = keep.tile([P, BATCH, N], BF16)
        shift_x = keep.tile([P, BATCH, N], F32)
        h_codes = keep.tile([P, PASSES * BATCH * P], U32, align_bytes=256)
        h_planes = keep.tile([P, PASSES * BATCH * P], U8, align_bytes=256)
        eps_col = keep.tile([P, 1], F32)
        warm = keep.tile([P, 1], F32)
        sums = keep.tile([P, BATCH, HALVES], F32)
        pivot = keep.tile([P, BATCH], F32)
        squares = keep.tile([P, HALF], BF16)
        sum_sq = keep.tile([P, BATCH, HALVES], F32)
        var_part = keep.tile([P, BATCH, HALVES], F32)
        neg_mean = keep.tile([P, BATCH], F32)
        gap_sq = keep.tile([P, BATCH], F32)
        rstd = keep.tile([P, BATCH], F32)

        w_planes = keep.tile([P, CHUNKS, N], U8, align_bytes=256)
        nc.vector.memset(eps_col[:], EPS)
        nc.vector.memset(w_planes[:].rearrange("p c n -> p (c n)").bitcast(I32), 0)
        nc.vector.memset(rows[:].rearrange("p v n -> p (v n)").bitcast(I32), 0)
        nc.vector.memset(ones[:], 1.0)
        make_identity(nc, ident[:])
        for v, vec in enumerate((proj_bias, norm_gain, norm_shift)):
            nc.scalar.dma_start(out=rows[0:1, v, :], in_=vec.unsqueeze(0))
        nc.scalar.activation(out=warm[:], in_=eps_col[:], func=ACT.Abs_reciprocal_sqrt)

        h_view = h_attn.rearrange("b s k -> s b k")
        h_raw = []
        w_sb = []

        def load_h(c):
            raw = h_pool.tile([P, BATCH, CHUNK * K_PASS], BF16, name="raw")
            k_cols = slice(c * CHUNK * K_PASS, (c + 1) * CHUNK * K_PASS)
            nc.sync.dma_start(out=raw[:], in_=h_view[:, :, k_cols])
            h_raw.append(raw)

        def load_scales(c):
            for q in range(QUADRANTS):
                nc.gpsimd.dma_start(
                    out=w_planes[32 * q : 32 * q + 4 * CHUNK, c, :].bitcast(F32),
                    in_=w_scales[CHUNK * c : CHUNK * (c + 1), 4 * q : 4 * q + 4, :].bitcast(F32),
                )

        def load_w(c):
            tiles = []
            for first in range(CHUNK * c, CHUNK * (c + 1), PAIR):
                words = w_pool.tile([P, PAIR, N], U32, name="words", align_bytes=256)
                tiles.append((first, words))
                for e in range(PAIR):
                    w_sb.append(words[:, e, :])
            if c < CHUNKS - 1:
                for g in range(CHUNK * c, CHUNK * (c + 1)):
                    nc.sync.dma_start(
                        out=w_sb[g].bitcast(I32), in_=w_words[g].rearrange("p n t -> p (n t)").bitcast(I32)
                    )
                    if g == CHUNK * c and c + H_AHEAD < CHUNKS:
                        load_h(c + H_AHEAD)
            else:
                for j in range(HALVES):
                    n_cols = slice(j * HALF, (j + 1) * HALF)
                    for first, words in tiles:
                        nc.sync.dma_start(
                            out=words[:, :, n_cols].bitcast(I32),
                            in_=w_words[first : first + PAIR, :, n_cols, :]
                            .rearrange("g p n t -> p g (n t)")
                            .bitcast(I32),
                        )

        for c in range(CHUNKS):
            load_scales(c)
        for c in range(H_AHEAD):
            load_h(c)
        for c in range(CHUNKS):
            load_w(c)
            if c == CHUNKS - 3:
                nc.sync.dma_start(out=x_sb[:], in_=x.rearrange("b s n -> s b n"))

        acc = [
            [acc_pool.tile([P, HALF], F32, name="acc%d%d" % (b, j)) for j in range(HALVES)]
            for b in range(BATCH)
        ]

        h_sorted = []

        def sort_chunk(c):
            by_parity = sorted_pool.tile([P, BATCH, CHUNK, 2, P], F32, name="by_parity")
            nc.vector.tensor_copy(
                out=by_parity[:],
                in_=h_raw[c][:].bitcast(F32).rearrange("p b (i w u) -> p b i u w", i=CHUNK, u=2),
            )
            h_sorted.append(by_parity)

        def transpose_chunk(c):
            grouped = grouped_pool.tile([P, CHUNK * BATCH * P * PACK], BF16, name="grouped", align_bytes=64)
            grouped_words = grouped[:].bitcast(F32)
            for i in range(CHUNK):
                bank = bank_pool.tile([P, HALF], F32, name="bank")
                for b in range(BATCH):
                    for u in range(2):
                        nc.tensor.transpose(
                            bank[:, (2 * b + u) * P : (2 * b + u + 1) * P],
                            h_sorted[c][:, b, i, u, :],
                            ident[:],
                        )
                nc.scalar.copy(
                    out=grouped_words[:, HALF * i : HALF * (i + 1)].rearrange(
                        "p (b s u) -> p b s u", b=BATCH, u=2
                    ),
                    in_=bank[:].rearrange("p (b u s) -> p b s u", b=BATCH, u=2),
                )
            return grouped

        def quantise_chunk(c, grouped):
            cols = slice(c * CHUNK * BATCH * P, (c + 1) * CHUNK * BATCH * P)
            nc.vector.quantize_mx(
                out=h_codes[:, cols].bitcast(FP8X4), scales=h_planes[:, cols], in_=grouped[:]
            )

        def multiply(g, b, j):
            rows_gb = slice((g * BATCH + b) * P, (g * BATCH + b + 1) * P)
            n_cols = slice(j * HALF, (j + 1) * HALF)
            nc.tensor.matmul_mx(
                out=acc[b][j][:],
                lhsT=h_codes[:, rows_gb].bitcast(FP8X4),
                lhsT_scale=h_planes[:, rows_gb],
                rhs=w_sb[g][:, n_cols].bitcast(FP8X4),
                rhs_scale=w_planes[4 * (g % CHUNK) : P, g // CHUNK, n_cols],
                start=(g == 0),
                stop=(g == PASSES - 1),
            )

        def multiply_chunk(c):
            for g in range(CHUNK * c, CHUNK * (c + 1)):
                for b in range(BATCH):
                    for j in range(HALVES):
                        multiply(g, b, j)

        def spread_row(v):
            for j in range(HALVES):
                n_cols = slice(j * HALF, (j + 1) * HALF)
                bank = bank_pool.tile([P, HALF], F32, name="bank")
                nc.tensor.matmul(bank[:], lhsT=ones[:], rhs=rows[:, v, n_cols], start=True, stop=True)
                nc.scalar.copy(out=spread[:, v, n_cols], in_=bank[:])

        def add_bias(b, j):
            n_cols = slice(j * HALF, (j + 1) * HALF)
            nc.vector.scalar_tensor_tensor(
                out=o[:, b, n_cols], in0=acc[b][j][:], scalar=1.0, in1=spread[:, 0, n_cols],
                op0=ALU.mult, op1=ALU.add, accum_out=sums[:, b, j : j + 1],
            )
            if j == 0:
                nc.vector.tensor_scalar_mul(
                    out=pivot[:, b : b + 1], in0=sums[:, b, 0:1], scalar1=1.0 / HALF
                )

        def add_squares(b, j):
            n_cols = slice(j * HALF, (j + 1) * HALF)
            nc.scalar.activation(
                out=squares[:], in_=o[:, b, n_cols], func=ACT.Square, bias=pivot[:, b : b + 1],
                scale=-1.0, accum_out=sum_sq[:, b, j : j + 1],
            )
            nc.scalar.activation(
                out=var_part[:, b, j : j + 1], in_=sum_sq[:, b, j : j + 1], func=ACT.Identity,
                bias=eps_col[:] if j == 0 else var_part[:, b, 0:1], scale=1.0 / N,
            )

        def add_mean(b):
            nc.vector.tensor_scalar(
                out=neg_mean[:, b : b + 1], in0=sums[:, b, 0:1], scalar1=sums[:, b, 1:2],
                scalar2=-1.0 / N, op0=ALU.add, op1=ALU.mult,
            )
            nc.scalar.activation(
                out=gap_sq[:, b : b + 1], in_=neg_mean[:, b : b + 1], func=ACT.Square,
                bias=pivot[:, b : b + 1], scale=1.0,
            )
            nc.scalar.activation(
                out=rstd[:, b : b + 1], in_=gap_sq[:, b : b + 1], func=ACT.Abs_reciprocal_sqrt,
                bias=var_part[:, b, 1:2], scale=-1.0,
            )

        def centre(b):
            nc.vector.scalar_tensor_tensor(
                out=centred[:, b, :], in0=o[:, b, :], scalar=neg_mean[:, b : b + 1],
                in1=spread[:, 1, :], op0=ALU.add, op1=ALU.mult,
            )

        def scale_and_store(b):
            for j in range(HALVES):
                n_cols = slice(j * HALF, (j + 1) * HALF)
                nc.vector.scalar_tensor_tensor(
                    out=centred[:, b, n_cols], in0=centred[:, b, n_cols], scalar=rstd[:, b : b + 1],
                    in1=shift_x[:, b, n_cols], op0=ALU.mult, op1=ALU.add,
                )
                nc.sync.dma_start(out=out[b, :, n_cols], in_=centred[:, b, n_cols])

        def prepare_chunk(c):
            grouped = transpose_chunk(c)
            if c + 1 < CHUNKS:
                sort_chunk(c + 1)
            quantise_chunk(c, grouped)

        last = CHUNKS - 1
        sort_chunk(0)
        for c in range(T_AHEAD):
            prepare_chunk(c)
        for v in range(3):
            spread_row(v)
        for c in range(last):
            if c + T_AHEAD < CHUNKS:
                prepare_chunk(c + T_AHEAD)
            multiply_chunk(c)
        for b in range(BATCH):
            nc.vector.tensor_tensor(
                out=shift_x[:, b, :], in0=spread[:, 2, :], in1=x_sb[:, b, :], op=ALU.add
            )

        o = sorted_pool.tile([P, BATCH, N], F32, name="by_parity")
        centred = sorted_pool.tile([P, BATCH, N], F32, name="by_parity")
        for j in range(HALVES):
            for b in range(BATCH):
                for g in range(CHUNK * last, PASSES):
                    multiply(g, b, j)
                add_bias(b, j)
                add_squares(b, j)
                if j == HALVES - 1:
                    add_mean(b)
        for b in range(BATCH):
            centre(b)
        for b in range(BATCH):
            scale_and_store(b)
